import numpy as np
import ml_dtypes

BF16 = ml_dtypes.bfloat16


def bf(x):
    return np.asarray(x, np.float32).astype(BF16)


def f32(x):
    return np.asarray(x, np.float32)


def f64(x):
    return np.asarray(x).astype(np.float64)


def striped(idx):
    return np.tile(idx.reshape(-1, 16).T, (8, 1))


C, S, B, K, T, D, M, N = 256, 2048, 2048, 4, 8, 512, 128, 16384


def crelu(v):
    return np.minimum(np.maximum(v, 0.0), 1.0)


def setup_inputs():
    bound1 = np.sqrt(6.0 / (M + D))
    boundo = np.sqrt(6.0 / (M + 1.0))
    return {"table": f32(0.35 * np.random.standard_normal((C, S))), "ft_bias": f32(0.1 * np.random.standard_normal((C, 1))), "stm": f32(np.random.uniform(0.0, 1.0, (1, B))), "w1": bf(np.random.uniform(-bound1, bound1, (D, M))), "b1": f32(0.1 * np.random.standard_normal((M, 1))), "wo": bf(np.random.uniform(-boundo, boundo, (M, 1))), "bo": f32(np.random.uniform(0.1, 0.3, (1, 1))), "offs": striped(np.concatenate([np.random.permutation(S) for _ in range(T)]))}


def reference(table, ft_bias, stm, w1, b1, wo, bo, offs):
    idx = offs[:16].T.reshape(-1)
    slots = idx.reshape(T, B)
    tab = f64(table)
    w_acc = f64(ft_bias) + sum(tab[:, slots[t]] for t in range(K))
    b_acc = f64(ft_bias) + sum(tab[:, slots[t]] for t in range(K, T))
    s = f64(stm)
    x = crelu(np.concatenate([s * w_acc + (1.0 - s) * b_acc, s * b_acc + (1.0 - s) * w_acc], axis=0))
    h = crelu(f64(w1).T @ x + f64(b1))
    return f64(wo).T @ h + f64(bo)

@@ -1,0 +1,116 @@
+import concourse.mybir as mybir
+from concourse.masks import make_identity
+
+P = 128
+C, S, B = 256, 2048, 2048
+SLOTS_PER_SIDE = 4
+D, M = 2 * C, 128
+BLOCKS = C // P
+BANK = 512
+CHUNKS = (512, 512, 512, 256, 128, 128)
+assert sum(CHUNKS) == B and max(CHUNKS) <= BANK
+PER_COLUMN = 16
+
+FLOPS = 2 * D * M * B + 2 * M * B
+
+F32, BF16, U16 = mybir.dt.float32, mybir.dt.bfloat16, mybir.dt.uint16
+ADD, SUBTRACT, MULT = mybir.AluOpType.add, mybir.AluOpType.subtract, mybir.AluOpType.mult
+RELU = mybir.ActivationFunctionType.Relu
+IDENTITY = mybir.ActivationFunctionType.Identity
+
+
+def gather_sum(nc, sums, window, offsets, bias_wide, slots, n0, width):
+    running = bias_wide
+    for t in slots:
+        first = (t * B + n0) // PER_COLUMN
+        picked = window[:].indirect(offsets[:, first : first + width // PER_COLUMN])
+        summed = sums.tile([P, width], F32, name="summed")
+        nc.vector.tensor_tensor(summed[:], picked, running[:, :width], ADD)
+        running = summed
+    return running
+
+
+def clip01(nc, work, clipped, value, one_minus_bias, width):
+    above = work.tile([P, width], F32, name="above")
+    nc.scalar.activation(above[:], value, RELU, bias=one_minus_bias, scale=-1.0)
+    nc.scalar.activation(clipped, above[:], RELU, bias=1.0, scale=-1.0)
+
+
+def tile_halfkpnnue_kernel(tc, table, ft_bias, stm, w1, b1, wo, bo, offs, out):
+    nc = tc.nc
+    with (
+        tc.tile_pool(name="held", bufs=1) as held,
+        tc.tile_pool(name="sums", bufs=8) as sums,
+        tc.tile_pool(name="work", bufs=3) as work,
+        tc.psum_pool(name="blend", bufs=3) as blend,
+        tc.psum_pool(name="layers", bufs=1) as layers,
+    ):
+        offsets = held.tile([P, offs.shape[1]], U16, name="offsets")
+        nc.sync.dma_start(offsets[:], offs)
+        windows = [held.tile([P, S], F32, name=f"window{k}") for k in range(BLOCKS)]
+        biases = [held.tile([P, 1], F32, name=f"bias{k}") for k in range(BLOCKS)]
+        for k in range(BLOCKS):
+            nc.scalar.dma_start(biases[k][:], ft_bias[k * P : (k + 1) * P, :])
+            nc.sync.dma_start(windows[k][:], table[k * P : (k + 1) * P, :])
+        stm_all = held.tile([P, B], F32, name="stm_all")
+        nc.sync.dma_start(stm_all[:], stm.to_broadcast([P, B]))
+        w1_sb = held.tile([P, D // P, M], BF16, name="w1_sb")
+        nc.sync.dma_start(w1_sb[:], w1.rearrange("(j p) m -> p j m", p=P))
+        b1_sb = held.tile([M, 1], F32, name="b1_sb")
+        nc.scalar.dma_start(b1_sb[:], b1)
+        wo_sb = held.tile([M, 1], BF16, name="wo_sb")
+        nc.scalar.dma_start(wo_sb[:], wo)
+        bo_sb = held.tile([1, 1], F32, name="bo_sb")
+        nc.scalar.dma_start(bo_sb[:], bo)
+
+        bias_wide = [held.tile([P, BANK], F32, name=f"bias_wide{k}") for k in range(BLOCKS)]
+        for k in range(BLOCKS):
+            nc.vector.tensor_copy(bias_wide[k][:], biases[k][:, 0:1].to_broadcast([P, BANK]))
+        plus = held.tile([P, P], F32, name="plus")
+        make_identity(nc, plus[:])
+        minus = held.tile([P, P], F32, name="minus")
+        nc.scalar.mul(minus[:], plus[:], -1.0)
+        one_minus_b1 = held.tile([M, 1], F32, name="one_minus_b1")
+        nc.scalar.activation(one_minus_b1[:], b1_sb[:], IDENTITY, bias=1.0, scale=-1.0)
+
+        score = held.tile([1, B], F32, name="score")
+
+        n0 = 0
+        for width in CHUNKS:
+            here = slice(n0, n0 + width)
+            hidden_ps = layers.tile([M, width], F32, name="hidden_ps")
+            for k in range(BLOCKS):
+                white = range(0, SLOTS_PER_SIDE)
+                black = range(SLOTS_PER_SIDE, 2 * SLOTS_PER_SIDE)
+                w_acc = gather_sum(nc, sums, windows[k], offsets, bias_wide[k], white, n0, width)
+                b_acc = gather_sum(nc, sums, windows[k], offsets, bias_wide[k], black, n0, width)
+
+                other_ps = blend.tile([P, width], F32, name="other_ps")
+                nc.tensor.matmul(other_ps[:], plus[:], w_acc[:], start=True, stop=False)
+                own_ps = blend.tile([P, width], F32, name="own_ps")
+                nc.tensor.matmul(own_ps[:], plus[:], b_acc[:], start=True, stop=False)
+                diff = work.tile([P, width], F32, name="diff")
+                nc.vector.tensor_tensor(diff[:], w_acc[:], b_acc[:], SUBTRACT)
+                e = work.tile([P, width], F32, name="e")
+                nc.vector.tensor_tensor(e[:], diff[:], stm_all[:, here], MULT)
+                nc.tensor.matmul(own_ps[:], plus[:], e[:], start=False, stop=True)
+                nc.tensor.matmul(other_ps[:], minus[:], e[:], start=False, stop=True)
+
+                for half, blended_ps in enumerate((own_ps, other_ps)):
+                    x = work.tile([P, width], BF16, name="x")
+                    clip01(nc, work, x[:], blended_ps[:], 1.0, width)
+                    nc.tensor.matmul(
+                        hidden_ps[:],
+                        w1_sb[:, half * BLOCKS + k, :],
+                        x[:],
+                        start=(k == 0 and half == 0),
+                        stop=(k == BLOCKS - 1 and half == 1),
+                    )
+
+            h = work.tile([M, width], BF16, name="h")
+            clip01(nc, work, h[:], hidden_ps[:], one_minus_b1[:, 0:1], width)
+            score_ps = layers.tile([1, width], F32, name="score_ps")
+            nc.tensor.matmul(score_ps[:], wo_sb[:, 0:1], h[:], start=True, stop=True)
+            nc.scalar.activation(score[:, here], score_ps[:], IDENTITY, bias=bo_sb[0:1, 0:1], scale=1.0)
+            nc.sync.dma_start(out[:, here], score[:, here])
+            n0 += width

@@ -6,28 +6,32 @@ C, S, B = 256, 2048, 2048
 SLOTS_PER_SIDE = 4
 D, M = 2 * C, 128
 BLOCKS = C // P
+GROUPS = B // P
 BANK = 512
 CHUNKS = (512, 512, 512, 256, 128, 128)
-assert sum(CHUNKS) == B and max(CHUNKS) <= BANK
+assert sum(CHUNKS) == B and max(CHUNKS) <= BANK and all(width % P == 0 for width in CHUNKS)
 PER_COLUMN = 16
 
 FLOPS = 2 * D * M * B + 2 * M * B
 
 F32, BF16, U16 = mybir.dt.float32, mybir.dt.bfloat16, mybir.dt.uint16
-ADD, SUBTRACT, MULT = mybir.AluOpType.add, mybir.AluOpType.subtract, mybir.AluOpType.mult
+ADD = mybir.AluOpType.add
 RELU = mybir.ActivationFunctionType.Relu
 IDENTITY = mybir.ActivationFunctionType.Identity
+COPY = mybir.ActivationFunctionType.Copy
 
 
-def gather_sum(nc, sums, window, offsets, bias_wide, slots, n0, width):
-    running = bias_wide
-    for t in slots:
-        first = (t * B + n0) // PER_COLUMN
-        picked = window[:].indirect(offsets[:, first : first + width // PER_COLUMN])
-        summed = sums.tile([P, width], F32, name="summed")
-        nc.vector.tensor_tensor(summed[:], picked, running[:, :width], ADD)
-        running = summed
-    return running
+def gather_sums(nc, sums, windows, offsets, bias_wide, n0, width):
+    acc = [[bias_wide[k], bias_wide[k]] for k in range(BLOCKS)]
+    for i in range(SLOTS_PER_SIDE):
+        for k in range(BLOCKS):
+            for side in range(2):
+                first = ((side * SLOTS_PER_SIDE + i) * B + n0) // PER_COLUMN
+                picked = windows[k][:].indirect(offsets[:, first : first + width // PER_COLUMN])
+                summed = sums.tile([P, width], F32, name="summed")
+                nc.vector.tensor_tensor(summed[:], picked, acc[k][side][:, :width], ADD)
+                acc[k][side] = summed
+    return acc
 
 
 def clip01(nc, work, clipped, value, one_minus_bias, width):
@@ -40,9 +44,10 @@ def tile_halfkpnnue_kernel(tc, table, ft_bias, stm, w1, b1, wo, bo, offs, out):
     nc = tc.nc
     with (
         tc.tile_pool(name="held", bufs=1) as held,
-        tc.tile_pool(name="sums", bufs=8) as sums,
+        tc.tile_pool(name="sums", bufs=12) as sums,
         tc.tile_pool(name="work", bufs=3) as work,
-        tc.psum_pool(name="blend", bufs=3) as blend,
+        tc.psum_pool(name="turned", bufs=2) as turned,
+        tc.psum_pool(name="blend", bufs=2) as blend,
         tc.psum_pool(name="layers", bufs=1) as layers,
     ):
         offsets = held.tile([P, offs.shape[1]], U16, name="offsets")
@@ -52,8 +57,8 @@ def tile_halfkpnnue_kernel(tc, table, ft_bias, stm, w1, b1, wo, bo, offs, out):
         for k in range(BLOCKS):
             nc.scalar.dma_start(biases[k][:], ft_bias[k * P : (k + 1) * P, :])
             nc.sync.dma_start(windows[k][:], table[k * P : (k + 1) * P, :])
-        stm_all = held.tile([P, B], F32, name="stm_all")
-        nc.sync.dma_start(stm_all[:], stm.to_broadcast([P, B]))
+        stm_rows = held.tile([GROUPS, P], F32, name="stm_rows")
+        nc.scalar.dma_start(stm_rows[:], stm.rearrange("o (g p) -> (o g) p", p=P))
         w1_sb = held.tile([P, D // P, M], BF16, name="w1_sb")
         nc.sync.dma_start(w1_sb[:], w1.rearrange("(j p) m -> p j m", p=P))
         b1_sb = held.tile([M, 1], F32, name="b1_sb")
@@ -66,35 +71,49 @@ def tile_halfkpnnue_kernel(tc, table, ft_bias, stm, w1, b1, wo, bo, offs, out):
         bias_wide = [held.tile([P, BANK], F32, name=f"bias_wide{k}") for k in range(BLOCKS)]
         for k in range(BLOCKS):
             nc.vector.tensor_copy(bias_wide[k][:], biases[k][:, 0:1].to_broadcast([P, BANK]))
-        plus = held.tile([P, P], F32, name="plus")
-        make_identity(nc, plus[:])
-        minus = held.tile([P, P], F32, name="minus")
-        nc.scalar.mul(minus[:], plus[:], -1.0)
+        identity = held.tile([P, P], F32, name="identity")
+        make_identity(nc, identity[:])
         one_minus_b1 = held.tile([M, 1], F32, name="one_minus_b1")
         nc.scalar.activation(one_minus_b1[:], b1_sb[:], IDENTITY, bias=1.0, scale=-1.0)
+        stm_ps = turned.tile([P, 2 * P], F32, name="turned_ps")
+        nc.tensor.matmul(stm_ps[:, 0:GROUPS], stm_rows[:], identity[0:GROUPS, 0:GROUPS], start=True, stop=True)
+        stm_col = held.tile([P, GROUPS], F32, name="stm_col")
+        nc.scalar.copy(stm_col[:], stm_ps[:, 0:GROUPS])
+        rest_col = held.tile([P, GROUPS], F32, name="rest_col")
+        nc.scalar.activation(rest_col[:], stm_ps[:, 0:GROUPS], IDENTITY, bias=1.0, scale=-1.0)
 
         score = held.tile([1, B], F32, name="score")
 
         n0 = 0
         for width in CHUNKS:
             here = slice(n0, n0 + width)
+            acc = gather_sums(nc, sums, windows, offsets, bias_wide, n0, width)
             hidden_ps = layers.tile([M, width], F32, name="hidden_ps")
             for k in range(BLOCKS):
-                white = range(0, SLOTS_PER_SIDE)
-                black = range(SLOTS_PER_SIDE, 2 * SLOTS_PER_SIDE)
-                w_acc = gather_sum(nc, sums, windows[k], offsets, bias_wide[k], white, n0, width)
-                b_acc = gather_sum(nc, sums, windows[k], offsets, bias_wide[k], black, n0, width)
-
-                other_ps = blend.tile([P, width], F32, name="other_ps")
-                nc.tensor.matmul(other_ps[:], plus[:], w_acc[:], start=True, stop=False)
+                w_acc, b_acc = acc[k]
                 own_ps = blend.tile([P, width], F32, name="own_ps")
-                nc.tensor.matmul(own_ps[:], plus[:], b_acc[:], start=True, stop=False)
-                diff = work.tile([P, width], F32, name="diff")
-                nc.vector.tensor_tensor(diff[:], w_acc[:], b_acc[:], SUBTRACT)
-                e = work.tile([P, width], F32, name="e")
-                nc.vector.tensor_tensor(e[:], diff[:], stm_all[:, here], MULT)
-                nc.tensor.matmul(own_ps[:], plus[:], e[:], start=False, stop=True)
-                nc.tensor.matmul(other_ps[:], minus[:], e[:], start=False, stop=True)
+                other_ps = blend.tile([P, width], F32, name="other_ps")
+                for g0 in range(0, width, P):
+                    group = (n0 + g0) // P
+                    cols = slice(g0, g0 + P)
+                    white, black = slice(0, P), slice(P, 2 * P)
+                    turned_ps = turned.tile([P, 2 * P], F32, name="turned_ps")
+                    nc.tensor.transpose(turned_ps[:, white], w_acc[:, cols], identity[:])
+                    nc.tensor.transpose(turned_ps[:, black], b_acc[:, cols], identity[:])
+                    by_stm = work.tile([P, 2 * P], F32, name="by_stm")
+                    nc.scalar.activation(by_stm[:], turned_ps[:], COPY, scale=stm_col[:, group : group + 1])
+                    by_rest = work.tile([P, 2 * P], F32, name="by_rest")
+                    nc.scalar.activation(by_rest[:], turned_ps[:], COPY, scale=rest_col[:, group : group + 1])
+                    for blended_ps, first, second in (
+                        (own_ps, by_stm[:, white], by_rest[:, black]),
+                        (other_ps, by_rest[:, white], by_stm[:, black]),
+                    ):
+                        nc.tensor.matmul(
+                            blended_ps[:, cols], first, identity[:], is_transpose=True, start=True, stop=False
+                        )
+                        nc.tensor.matmul(
+                            blended_ps[:, cols], second, identity[:], is_transpose=True, start=False, stop=True
+                        )
 
                 for half, blended_ps in enumerate((own_ps, other_ps)):
                     x = work.tile([P, width], BF16, name="x")

@@ -21,16 +21,15 @@ IDENTITY = mybir.ActivationFunctionType.Identity
 COPY = mybir.ActivationFunctionType.Copy
 
 
-def gather_sums(nc, sums, windows, offsets, bias_wide, n0, width):
-    acc = [[bias_wide[k], bias_wide[k]] for k in range(BLOCKS)]
+def gather_sums(nc, sums, window, offsets, bias_wide, n0, width):
+    acc = [bias_wide, bias_wide]
     for i in range(SLOTS_PER_SIDE):
-        for k in range(BLOCKS):
-            for side in range(2):
-                first = ((side * SLOTS_PER_SIDE + i) * B + n0) // PER_COLUMN
-                picked = windows[k][:].indirect(offsets[:, first : first + width // PER_COLUMN])
-                summed = sums.tile([P, width], F32, name="summed")
-                nc.vector.tensor_tensor(summed[:], picked, acc[k][side][:, :width], ADD)
-                acc[k][side] = summed
+        for side in range(2):
+            first = ((side * SLOTS_PER_SIDE + i) * B + n0) // PER_COLUMN
+            picked = window[:].indirect(offsets[:, first : first + width // PER_COLUMN])
+            summed = sums.tile([P, width], F32, name="summed")
+            nc.vector.tensor_tensor(summed[:], picked, acc[side][:, :width], ADD)
+            acc[side] = summed
     return acc
 
 
@@ -44,7 +43,7 @@ def tile_halfkpnnue_kernel(tc, table, ft_bias, stm, w1, b1, wo, bo, offs, out):
     nc = tc.nc
     with (
         tc.tile_pool(name="held", bufs=1) as held,
-        tc.tile_pool(name="sums", bufs=12) as sums,
+        tc.tile_pool(name="sums", bufs=8) as sums,
         tc.tile_pool(name="work", bufs=3) as work,
         tc.psum_pool(name="turned", bufs=2) as turned,
         tc.psum_pool(name="blend", bufs=2) as blend,
@@ -87,10 +86,9 @@ def tile_halfkpnnue_kernel(tc, table, ft_bias, stm, w1, b1, wo, bo, offs, out):
         n0 = 0
         for width in CHUNKS:
             here = slice(n0, n0 + width)
-            acc = gather_sums(nc, sums, windows, offsets, bias_wide, n0, width)
             hidden_ps = layers.tile([M, width], F32, name="hidden_ps")
             for k in range(BLOCKS):
-                w_acc, b_acc = acc[k]
+                w_acc, b_acc = gather_sums(nc, sums, windows[k], offsets, bias_wide[k], n0, width)
                 own_ps = blend.tile([P, width], F32, name="own_ps")
                 other_ps = blend.tile([P, width], F32, name="other_ps")
                 for g0 in range(0, width, P):

@@ -33,10 +33,12 @@ def gather_sums(nc, sums, window, offsets, bias_wide, n0, width):
     return acc
 
 
-def clip01(nc, work, clipped, value, one_minus_bias, width):
-    above = work.tile([P, width], F32, name="above")
-    nc.scalar.activation(above[:], value, RELU, bias=one_minus_bias, scale=-1.0)
-    nc.scalar.activation(clipped, above[:], RELU, bias=1.0, scale=-1.0)
+def clip01(nc, work, clipped, value_ps, one_minus_bias, columns):
+    above = work.tile([P, columns], F32, name="above")
+    for c0 in range(0, columns, BANK):
+        piece = slice(c0, min(c0 + BANK, columns))
+        nc.scalar.activation(above[:, piece], value_ps[:, piece], RELU, bias=one_minus_bias, scale=-1.0)
+    nc.scalar.activation(clipped[:], above[:], RELU, bias=1.0, scale=-1.0)
 
 
 def tile_halfkpnnue_kernel(tc, table, ft_bias, stm, w1, b1, wo, bo, offs, out):
@@ -89,8 +91,7 @@ def tile_halfkpnnue_kernel(tc, table, ft_bias, stm, w1, b1, wo, bo, offs, out):
             hidden_ps = layers.tile([M, width], F32, name="hidden_ps")
             for k in range(BLOCKS):
                 w_acc, b_acc = gather_sums(nc, sums, windows[k], offsets, bias_wide[k], n0, width)
-                own_ps = blend.tile([P, width], F32, name="own_ps")
-                other_ps = blend.tile([P, width], F32, name="other_ps")
+                blended_ps = blend.tile([P, 2 * width], F32, name="blended_ps")
                 for g0 in range(0, width, P):
                     group = (n0 + g0) // P
                     cols = slice(g0, g0 + P)
@@ -102,30 +103,30 @@ def tile_halfkpnnue_kernel(tc, table, ft_bias, stm, w1, b1, wo, bo, offs, out):
                     nc.scalar.activation(by_stm[:], turned_ps[:], COPY, scale=stm_col[:, group : group + 1])
                     by_rest = work.tile([P, 2 * P], F32, name="by_rest")
                     nc.scalar.activation(by_rest[:], turned_ps[:], COPY, scale=rest_col[:, group : group + 1])
-                    for blended_ps, first, second in (
-                        (own_ps, by_stm[:, white], by_rest[:, black]),
-                        (other_ps, by_rest[:, white], by_stm[:, black]),
+                    for half, (first, second) in enumerate(
+                        ((by_stm[:, white], by_rest[:, black]), (by_rest[:, white], by_stm[:, black]))
                     ):
+                        there = slice(half * width + g0, half * width + g0 + P)
                         nc.tensor.matmul(
-                            blended_ps[:, cols], first, identity[:], is_transpose=True, start=True, stop=False
+                            blended_ps[:, there], first, identity[:], is_transpose=True, start=True, stop=False
                         )
                         nc.tensor.matmul(
-                            blended_ps[:, cols], second, identity[:], is_transpose=True, start=False, stop=True
+                            blended_ps[:, there], second, identity[:], is_transpose=True, start=False, stop=True
                         )
 
-                for half, blended_ps in enumerate((own_ps, other_ps)):
-                    x = work.tile([P, width], BF16, name="x")
-                    clip01(nc, work, x[:], blended_ps[:], 1.0, width)
+                x = work.tile([P, 2 * width], BF16, name="x")
+                clip01(nc, work, x, blended_ps, 1.0, 2 * width)
+                for half in range(2):
                     nc.tensor.matmul(
                         hidden_ps[:],
                         w1_sb[:, half * BLOCKS + k, :],
-                        x[:],
+                        x[:, half * width : (half + 1) * width],
                         start=(k == 0 and half == 0),
                         stop=(k == BLOCKS - 1 and half == 1),
                     )
 
             h = work.tile([M, width], BF16, name="h")
-            clip01(nc, work, h[:], hidden_ps[:], one_minus_b1[:, 0:1], width)
+            clip01(nc, work, h, hidden_ps, one_minus_b1[:, 0:1], width)
             score_ps = layers.tile([1, width], F32, name="score_ps")
             nc.tensor.matmul(score_ps[:], wo_sb[:, 0:1], h[:], start=True, stop=True)
             nc.scalar.activation(score[:, here], score_ps[:], IDENTITY, bias=bo_sb[0:1, 0:1], scale=1.0)

@@ -33,20 +33,20 @@ def gather_sums(nc, sums, window, offsets, bias_wide, n0, width):
     return acc
 
 
-def clip01(nc, work, clipped, value_ps, one_minus_bias, columns):
-    above = work.tile([P, columns], F32, name="above")
-    for c0 in range(0, columns, BANK):
-        piece = slice(c0, min(c0 + BANK, columns))
-        nc.scalar.activation(above[:, piece], value_ps[:, piece], RELU, bias=one_minus_bias, scale=-1.0)
-    nc.scalar.activation(clipped[:], above[:], RELU, bias=1.0, scale=-1.0)
+def clip01(nc, work, clipped, values, one_minus_bias, width):
+    aboves = [work.tile([P, width], F32, name="above") for value in values]
+    for above, value in zip(aboves, values):
+        nc.scalar.activation(above[:], value[:], RELU, bias=one_minus_bias, scale=-1.0)
+    for above, result in zip(aboves, clipped):
+        nc.scalar.activation(result[:], above[:], RELU, bias=1.0, scale=-1.0)
 
 
 def tile_halfkpnnue_kernel(tc, table, ft_bias, stm, w1, b1, wo, bo, offs, out):
     nc = tc.nc
     with (
         tc.tile_pool(name="held", bufs=1) as held,
-        tc.tile_pool(name="sums", bufs=8) as sums,
-        tc.tile_pool(name="work", bufs=3) as work,
+        tc.tile_pool(name="sums", bufs=12) as sums,
+        tc.tile_pool(name="work", bufs=4) as work,
         tc.psum_pool(name="turned", bufs=2) as turned,
         tc.psum_pool(name="blend", bufs=2) as blend,
         tc.psum_pool(name="layers", bufs=1) as layers,
@@ -91,7 +91,8 @@ def tile_halfkpnnue_kernel(tc, table, ft_bias, stm, w1, b1, wo, bo, offs, out):
             hidden_ps = layers.tile([M, width], F32, name="hidden_ps")
             for k in range(BLOCKS):
                 w_acc, b_acc = gather_sums(nc, sums, windows[k], offsets, bias_wide[k], n0, width)
-                blended_ps = blend.tile([P, 2 * width], F32, name="blended_ps")
+                own_ps = blend.tile([P, width], F32, name="own_ps")
+                other_ps = blend.tile([P, width], F32, name="other_ps")
                 for g0 in range(0, width, P):
                     group = (n0 + g0) // P
                     cols = slice(g0, g0 + P)
@@ -103,30 +104,30 @@ def tile_halfkpnnue_kernel(tc, table, ft_bias, stm, w1, b1, wo, bo, offs, out):
                     nc.scalar.activation(by_stm[:], turned_ps[:], COPY, scale=stm_col[:, group : group + 1])
                     by_rest = work.tile([P, 2 * P], F32, name="by_rest")
                     nc.scalar.activation(by_rest[:], turned_ps[:], COPY, scale=rest_col[:, group : group + 1])
-                    for half, (first, second) in enumerate(
-                        ((by_stm[:, white], by_rest[:, black]), (by_rest[:, white], by_stm[:, black]))
+                    for blended_ps, first, second in (
+                        (own_ps, by_stm[:, white], by_rest[:, black]),
+                        (other_ps, by_rest[:, white], by_stm[:, black]),
                     ):
-                        there = slice(half * width + g0, half * width + g0 + P)
                         nc.tensor.matmul(
-                            blended_ps[:, there], first, identity[:], is_transpose=True, start=True, stop=False
+                            blended_ps[:, cols], first, identity[:], is_transpose=True, start=True, stop=False
                         )
                         nc.tensor.matmul(
-                            blended_ps[:, there], second, identity[:], is_transpose=True, start=False, stop=True
+                            blended_ps[:, cols], second, identity[:], is_transpose=True, start=False, stop=True
                         )
 
-                x = work.tile([P, 2 * width], BF16, name="x")
-                clip01(nc, work, x, blended_ps, 1.0, 2 * width)
+                x = [work.tile([P, width], BF16, name="x") for half in range(2)]
+                clip01(nc, work, x, (own_ps, other_ps), 1.0, width)
                 for half in range(2):
                     nc.tensor.matmul(
                         hidden_ps[:],
                         w1_sb[:, half * BLOCKS + k, :],
-                        x[:, half * width : (half + 1) * width],
+                        x[half][:],
                         start=(k == 0 and half == 0),
                         stop=(k == BLOCKS - 1 and half == 1),
                     )
 
             h = work.tile([M, width], BF16, name="h")
-            clip01(nc, work, h, hidden_ps, one_minus_b1[:, 0:1], width)
+            clip01(nc, work, [h], [hidden_ps], one_minus_b1[:, 0:1], width)
             score_ps = layers.tile([1, width], F32, name="score_ps")
             nc.tensor.matmul(score_ps[:], wo_sb[:, 0:1], h[:], start=True, stop=True)
             nc.scalar.activation(score[:, here], score_ps[:], IDENTITY, bias=bo_sb[0:1, 0:1], scale=1.0)

@@ -10,12 +10,13 @@ GROUPS = B // P
 BANK = 512
 CHUNKS = (512, 512, 512, 256, 128, 128)
 assert sum(CHUNKS) == B and max(CHUNKS) <= BANK and all(width % P == 0 for width in CHUNKS)
+LAST = CHUNKS[-1]
 PER_COLUMN = 16
 
 FLOPS = 2 * D * M * B + 2 * M * B
 
 F32, BF16, U16 = mybir.dt.float32, mybir.dt.bfloat16, mybir.dt.uint16
-ADD = mybir.AluOpType.add
+ADD, MAX, MIN = mybir.AluOpType.add, mybir.AluOpType.max, mybir.AluOpType.min
 RELU = mybir.ActivationFunctionType.Relu
 IDENTITY = mybir.ActivationFunctionType.Identity
 COPY = mybir.ActivationFunctionType.Copy
@@ -68,6 +69,8 @@ def tile_halfkpnnue_kernel(tc, table, ft_bias, stm, w1, b1, wo, bo, offs, out):
         nc.scalar.dma_start(wo_sb[:], wo)
         bo_sb = held.tile([1, 1], F32, name="bo_sb")
         nc.scalar.dma_start(bo_sb[:], bo)
+        stm_wide = held.tile([P, LAST], F32, name="stm_wide")
+        nc.sync.dma_start(stm_wide[:], stm[:, B - LAST : B].to_broadcast([P, LAST]))
 
         bias_wide = [held.tile([P, BANK], F32, name=f"bias_wide{k}") for k in range(BLOCKS)]
         for k in range(BLOCKS):
@@ -91,6 +94,8 @@ def tile_halfkpnnue_kernel(tc, table, ft_bias, stm, w1, b1, wo, bo, offs, out):
             hidden_ps = layers.tile([M, width], F32, name="hidden_ps")
             for k in range(BLOCKS):
                 w_acc, b_acc = gather_sums(nc, sums, windows[k], offsets, bias_wide[k], n0, width)
+                if n0 + width == B and k == BLOCKS - 1:
+                    break
                 own_ps = blend.tile([P, width], F32, name="own_ps")
                 other_ps = blend.tile([P, width], F32, name="other_ps")
                 for g0 in range(0, width, P):
@@ -127,9 +132,30 @@ def tile_halfkpnnue_kernel(tc, table, ft_bias, stm, w1, b1, wo, bo, offs, out):
                     )
 
             h = work.tile([M, width], BF16, name="h")
-            clip01(nc, work, [h], [hidden_ps], one_minus_b1[:, 0:1], width)
             score_ps = layers.tile([1, width], F32, name="score_ps")
-            nc.tensor.matmul(score_ps[:], wo_sb[:, 0:1], h[:], start=True, stop=True)
-            nc.scalar.activation(score[:, here], score_ps[:], IDENTITY, bias=bo_sb[0:1, 0:1], scale=1.0)
+            if n0 + width < B:
+                clip01(nc, work, [h], [hidden_ps], one_minus_b1[:, 0:1], width)
+                nc.tensor.matmul(score_ps[:], wo_sb[:, 0:1], h[:], start=True, stop=True)
+                nc.scalar.activation(score[:, here], score_ps[:], IDENTITY, bias=bo_sb[0:1, 0:1], scale=1.0)
+            else:
+                k = BLOCKS - 1
+                gap = work.tile([P, LAST], F32, name="gap")
+                nc.vector.tensor_sub(gap[:], w_acc[:], b_acc[:])
+                shift = work.tile([P, LAST], F32, name="shift")
+                nc.vector.tensor_mul(shift[:], gap[:], stm_wide[:])
+                blended = work.tile([P, 2, LAST], F32, name="blended")
+                nc.vector.tensor_add(blended[:, 0, :], b_acc[:], shift[:])
+                nc.vector.tensor_sub(blended[:, 1, :], w_acc[:], shift[:])
+                x_last = work.tile([P, 2, LAST], BF16, name="x_last")
+                nc.vector.tensor_scalar(x_last[:], blended[:], 0.0, 1.0, MAX, MIN)
+                for half in range(2):
+                    nc.tensor.matmul(
+                        hidden_ps[:], w1_sb[:, half * BLOCKS + k, :], x_last[:, half, :], start=False, stop=(half == 1)
+                    )
+                floored = work.tile([M, LAST], F32, name="floored")
+                nc.vector.tensor_scalar(floored[:], hidden_ps[:], b1_sb[:, 0:1], 0.0, ADD, MAX)
+                nc.vector.tensor_scalar_min(h[:], floored[:], 1.0)
+                nc.tensor.matmul(score_ps[:], wo_sb[:, 0:1], h[:], start=True, stop=True)
+                nc.vector.tensor_scalar_add(score[:, here], score_ps[:], bo_sb[0:1, 0:1])
             nc.sync.dma_start(out[:, here], score[:, here])
             n0 += width

@@ -8,9 +8,9 @@ D, M = 2 * C, 128
 BLOCKS = C // P
 GROUPS = B // P
 BANK = 512
-CHUNKS = (512, 512, 512, 256, 128, 128)
-assert sum(CHUNKS) == B and max(CHUNKS) <= BANK and all(width % P == 0 for width in CHUNKS)
-LAST = CHUNKS[-1]
+CHUNKS = (1024, 512, 256, 128, 128)
+WIDEST, LAST = CHUNKS[0], CHUNKS[-1]
+assert sum(CHUNKS) == B and all(width % P == 0 and width <= WIDEST for width in CHUNKS)
 PER_COLUMN = 16
 
 FLOPS = 2 * D * M * B + 2 * M * B
@@ -37,9 +37,9 @@ def gather_sums(nc, sums, window, offsets, bias_wide, n0, width):
 def clip01(nc, work, clipped, values, one_minus_bias, width):
     aboves = [work.tile([P, width], F32, name="above") for value in values]
     for above, value in zip(aboves, values):
-        nc.scalar.activation(above[:], value[:], RELU, bias=one_minus_bias, scale=-1.0)
+        nc.scalar.activation(above[:], value, RELU, bias=one_minus_bias, scale=-1.0)
     for above, result in zip(aboves, clipped):
-        nc.scalar.activation(result[:], above[:], RELU, bias=1.0, scale=-1.0)
+        nc.scalar.activation(result, above[:], RELU, bias=1.0, scale=-1.0)
 
 
 def tile_halfkpnnue_kernel(tc, table, ft_bias, stm, w1, b1, wo, bo, offs, out):
@@ -55,10 +55,10 @@ def tile_halfkpnnue_kernel(tc, table, ft_bias, stm, w1, b1, wo, bo, offs, out):
         offsets = held.tile([P, offs.shape[1]], U16, name="offsets")
         nc.sync.dma_start(offsets[:], offs)
         windows = [held.tile([P, S], F32, name=f"window{k}") for k in range(BLOCKS)]
-        biases = [held.tile([P, 1], F32, name=f"bias{k}") for k in range(BLOCKS)]
         for k in range(BLOCKS):
-            nc.scalar.dma_start(biases[k][:], ft_bias[k * P : (k + 1) * P, :])
             nc.sync.dma_start(windows[k][:], table[k * P : (k + 1) * P, :])
+        biases = held.tile([P, BLOCKS], F32, name="biases")
+        nc.scalar.dma_start(biases[:], ft_bias.rearrange("(k p) o -> p (k o)", p=P))
         stm_rows = held.tile([GROUPS, P], F32, name="stm_rows")
         nc.scalar.dma_start(stm_rows[:], stm.rearrange("o (g p) -> (o g) p", p=P))
         w1_sb = held.tile([P, D // P, M], BF16, name="w1_sb")
@@ -72,9 +72,9 @@ def tile_halfkpnnue_kernel(tc, table, ft_bias, stm, w1, b1, wo, bo, offs, out):
         stm_wide = held.tile([P, LAST], F32, name="stm_wide")
         nc.sync.dma_start(stm_wide[:], stm[:, B - LAST : B].to_broadcast([P, LAST]))
 
-        bias_wide = [held.tile([P, BANK], F32, name=f"bias_wide{k}") for k in range(BLOCKS)]
+        bias_wide = [held.tile([P, WIDEST], F32, name=f"bias_wide{k}") for k in range(BLOCKS)]
         for k in range(BLOCKS):
-            nc.vector.tensor_copy(bias_wide[k][:], biases[k][:, 0:1].to_broadcast([P, BANK]))
+            nc.scalar.copy(bias_wide[k][:], biases[:, k : k + 1].to_broadcast([P, WIDEST]))
         identity = held.tile([P, P], F32, name="identity")
         make_identity(nc, identity[:])
         one_minus_b1 = held.tile([M, 1], F32, name="one_minus_b1")
@@ -86,76 +86,73 @@ def tile_halfkpnnue_kernel(tc, table, ft_bias, stm, w1, b1, wo, bo, offs, out):
         rest_col = held.tile([P, GROUPS], F32, name="rest_col")
         nc.scalar.activation(rest_col[:], stm_ps[:, 0:GROUPS], IDENTITY, bias=1.0, scale=-1.0)
 
+        x = held.tile([P, D // P, B], BF16, name="x")
         score = held.tile([1, B], F32, name="score")
 
-        n0 = 0
-        for width in CHUNKS:
+        def blend_and_clip(k, w_acc, b_acc, n0, width):
+            own_ps = blend.tile([P, width], F32, name="own_ps")
+            other_ps = blend.tile([P, width], F32, name="other_ps")
+            for g0 in range(0, width, P):
+                group = (n0 + g0) // P
+                cols = slice(g0, g0 + P)
+                white, black = slice(0, P), slice(P, 2 * P)
+                turned_ps = turned.tile([P, 2 * P], F32, name="turned_ps")
+                nc.tensor.transpose(turned_ps[:, white], w_acc[:, cols], identity[:])
+                nc.tensor.transpose(turned_ps[:, black], b_acc[:, cols], identity[:])
+                by_stm = work.tile([P, 2 * P], F32, name="by_stm")
+                nc.scalar.activation(by_stm[:], turned_ps[:], COPY, scale=stm_col[:, group : group + 1])
+                by_rest = work.tile([P, 2 * P], F32, name="by_rest")
+                nc.scalar.activation(by_rest[:], turned_ps[:], COPY, scale=rest_col[:, group : group + 1])
+                for blended_ps, first, second in (
+                    (own_ps, by_stm[:, white], by_rest[:, black]),
+                    (other_ps, by_rest[:, white], by_stm[:, black]),
+                ):
+                    nc.tensor.matmul(blended_ps[:, cols], first, identity[:], is_transpose=True, start=True, stop=False)
+                    nc.tensor.matmul(blended_ps[:, cols], second, identity[:], is_transpose=True, start=False, stop=True)
+            here = slice(n0, n0 + width)
+            clip01(nc, work, (x[:, k, here], x[:, BLOCKS + k, here]), (own_ps[:], other_ps[:]), 1.0, width)
+
+        def blend_and_clip_on_vector(k, w_acc, b_acc):
+            gap = work.tile([P, LAST], F32, name="gap")
+            nc.vector.tensor_sub(gap[:], w_acc[:], b_acc[:])
+            shift = work.tile([P, LAST], F32, name="shift")
+            nc.vector.tensor_mul(shift[:], gap[:], stm_wide[:])
+            blended = work.tile([P, 2, LAST], F32, name="blended")
+            nc.vector.tensor_add(blended[:, 0, :], b_acc[:], shift[:])
+            nc.vector.tensor_sub(blended[:, 1, :], w_acc[:], shift[:])
+            nc.vector.tensor_scalar(x[:, k : D // P : BLOCKS, B - LAST : B], blended[:], 0.0, 1.0, MAX, MIN)
+
+        def layers_and_store(n0, width, on_vector):
             here = slice(n0, n0 + width)
             hidden_ps = layers.tile([M, width], F32, name="hidden_ps")
-            for k in range(BLOCKS):
-                w_acc, b_acc = gather_sums(nc, sums, windows[k], offsets, bias_wide[k], n0, width)
-                if n0 + width == B and k == BLOCKS - 1:
-                    break
-                own_ps = blend.tile([P, width], F32, name="own_ps")
-                other_ps = blend.tile([P, width], F32, name="other_ps")
-                for g0 in range(0, width, P):
-                    group = (n0 + g0) // P
-                    cols = slice(g0, g0 + P)
-                    white, black = slice(0, P), slice(P, 2 * P)
-                    turned_ps = turned.tile([P, 2 * P], F32, name="turned_ps")
-                    nc.tensor.transpose(turned_ps[:, white], w_acc[:, cols], identity[:])
-                    nc.tensor.transpose(turned_ps[:, black], b_acc[:, cols], identity[:])
-                    by_stm = work.tile([P, 2 * P], F32, name="by_stm")
-                    nc.scalar.activation(by_stm[:], turned_ps[:], COPY, scale=stm_col[:, group : group + 1])
-                    by_rest = work.tile([P, 2 * P], F32, name="by_rest")
-                    nc.scalar.activation(by_rest[:], turned_ps[:], COPY, scale=rest_col[:, group : group + 1])
-                    for blended_ps, first, second in (
-                        (own_ps, by_stm[:, white], by_rest[:, black]),
-                        (other_ps, by_rest[:, white], by_stm[:, black]),
-                    ):
-                        nc.tensor.matmul(
-                            blended_ps[:, cols], first, identity[:], is_transpose=True, start=True, stop=False
-                        )
-                        nc.tensor.matmul(
-                            blended_ps[:, cols], second, identity[:], is_transpose=True, start=False, stop=True
-                        )
-
-                x = [work.tile([P, width], BF16, name="x") for half in range(2)]
-                clip01(nc, work, x, (own_ps, other_ps), 1.0, width)
-                for half in range(2):
-                    nc.tensor.matmul(
-                        hidden_ps[:],
-                        w1_sb[:, half * BLOCKS + k, :],
-                        x[half][:],
-                        start=(k == 0 and half == 0),
-                        stop=(k == BLOCKS - 1 and half == 1),
-                    )
-
+            for j in range(D // P):
+                nc.tensor.matmul(hidden_ps[:], w1_sb[:, j, :], x[:, j, here], start=(j == 0), stop=(j == D // P - 1))
             h = work.tile([M, width], BF16, name="h")
             score_ps = layers.tile([1, width], F32, name="score_ps")
-            if n0 + width < B:
-                clip01(nc, work, [h], [hidden_ps], one_minus_b1[:, 0:1], width)
-                nc.tensor.matmul(score_ps[:], wo_sb[:, 0:1], h[:], start=True, stop=True)
-                nc.scalar.activation(score[:, here], score_ps[:], IDENTITY, bias=bo_sb[0:1, 0:1], scale=1.0)
-            else:
-                k = BLOCKS - 1
-                gap = work.tile([P, LAST], F32, name="gap")
-                nc.vector.tensor_sub(gap[:], w_acc[:], b_acc[:])
-                shift = work.tile([P, LAST], F32, name="shift")
-                nc.vector.tensor_mul(shift[:], gap[:], stm_wide[:])
-                blended = work.tile([P, 2, LAST], F32, name="blended")
-                nc.vector.tensor_add(blended[:, 0, :], b_acc[:], shift[:])
-                nc.vector.tensor_sub(blended[:, 1, :], w_acc[:], shift[:])
-                x_last = work.tile([P, 2, LAST], BF16, name="x_last")
-                nc.vector.tensor_scalar(x_last[:], blended[:], 0.0, 1.0, MAX, MIN)
-                for half in range(2):
-                    nc.tensor.matmul(
-                        hidden_ps[:], w1_sb[:, half * BLOCKS + k, :], x_last[:, half, :], start=False, stop=(half == 1)
-                    )
-                floored = work.tile([M, LAST], F32, name="floored")
+            if on_vector:
+                floored = work.tile([M, width], F32, name="floored")
                 nc.vector.tensor_scalar(floored[:], hidden_ps[:], b1_sb[:, 0:1], 0.0, ADD, MAX)
                 nc.vector.tensor_scalar_min(h[:], floored[:], 1.0)
                 nc.tensor.matmul(score_ps[:], wo_sb[:, 0:1], h[:], start=True, stop=True)
                 nc.vector.tensor_scalar_add(score[:, here], score_ps[:], bo_sb[0:1, 0:1])
+            else:
+                clip01(nc, work, [h[:]], [hidden_ps[:]], one_minus_b1[:, 0:1], width)
+                nc.tensor.matmul(score_ps[:], wo_sb[:, 0:1], h[:], start=True, stop=True)
+                nc.scalar.activation(score[:, here], score_ps[:], IDENTITY, bias=bo_sb[0:1, 0:1], scale=1.0)
             nc.sync.dma_start(out[:, here], score[:, here])
-            n0 += width
+
+        n0 = 0
+        for chunk in CHUNKS:
+            for k in range(BLOCKS):
+                w_acc, b_acc = gather_sums(nc, sums, windows[k], offsets, bias_wide[k], n0, chunk)
+                very_last = n0 + chunk == B and k == BLOCKS - 1
+                if very_last:
+                    blend_and_clip_on_vector(k, w_acc, b_acc)
+                for a0 in range(0, chunk, BANK):
+                    width = min(BANK, chunk - a0)
+                    piece = slice(a0, a0 + width)
+                    if not very_last:
+                        blend_and_clip(k, w_acc[:, piece], b_acc[:, piece], n0 + a0, width)
+                    if k == BLOCKS - 1:
+                        layers_and_store(n0 + a0, width, very_last)
+            n0 += chunk

@@ -8,7 +8,7 @@ D, M = 2 * C, 128
 BLOCKS = C // P
 GROUPS = B // P
 BANK = 512
-CHUNKS = (1024, 512, 256, 128, 128)
+CHUNKS = (1024, 640, 384)
 WIDEST, LAST = CHUNKS[0], CHUNKS[-1]
 assert sum(CHUNKS) == B and all(width % P == 0 and width <= WIDEST for width in CHUNKS)
 PER_COLUMN = 16

@@ -48,9 +48,6 @@ def tile_halfkpnnue_kernel(tc, table, ft_bias, stm, w1, b1, wo, bo, offs, out):
         tc.tile_pool(name="held", bufs=1) as held,
         tc.tile_pool(name="sums", bufs=12) as sums,
         tc.tile_pool(name="work", bufs=4) as work,
-        tc.psum_pool(name="turned", bufs=2) as turned,
-        tc.psum_pool(name="blend", bufs=2) as blend,
-        tc.psum_pool(name="layers", bufs=1) as layers,
     ):
         offsets = held.tile([P, offs.shape[1]], U16, name="offsets")
         nc.sync.dma_start(offsets[:], offs)
@@ -79,80 +76,109 @@ def tile_halfkpnnue_kernel(tc, table, ft_bias, stm, w1, b1, wo, bo, offs, out):
         make_identity(nc, identity[:])
         one_minus_b1 = held.tile([M, 1], F32, name="one_minus_b1")
         nc.scalar.activation(one_minus_b1[:], b1_sb[:], IDENTITY, bias=1.0, scale=-1.0)
-        stm_ps = turned.tile([P, 2 * P], F32, name="turned_ps")
-        nc.tensor.matmul(stm_ps[:, 0:GROUPS], stm_rows[:], identity[0:GROUPS, 0:GROUPS], start=True, stop=True)
-        stm_col = held.tile([P, GROUPS], F32, name="stm_col")
-        nc.scalar.copy(stm_col[:], stm_ps[:, 0:GROUPS])
-        rest_col = held.tile([P, GROUPS], F32, name="rest_col")
-        nc.scalar.activation(rest_col[:], stm_ps[:, 0:GROUPS], IDENTITY, bias=1.0, scale=-1.0)
 
         x = held.tile([P, D // P, B], BF16, name="x")
         score = held.tile([1, B], F32, name="score")
 
-        def blend_and_clip(k, w_acc, b_acc, n0, width):
-            own_ps = blend.tile([P, width], F32, name="own_ps")
-            other_ps = blend.tile([P, width], F32, name="other_ps")
-            for g0 in range(0, width, P):
-                group = (n0 + g0) // P
-                cols = slice(g0, g0 + P)
-                white, black = slice(0, P), slice(P, 2 * P)
-                turned_ps = turned.tile([P, 2 * P], F32, name="turned_ps")
-                nc.tensor.transpose(turned_ps[:, white], w_acc[:, cols], identity[:])
-                nc.tensor.transpose(turned_ps[:, black], b_acc[:, cols], identity[:])
-                by_stm = work.tile([P, 2 * P], F32, name="by_stm")
-                nc.scalar.activation(by_stm[:], turned_ps[:], COPY, scale=stm_col[:, group : group + 1])
-                by_rest = work.tile([P, 2 * P], F32, name="by_rest")
-                nc.scalar.activation(by_rest[:], turned_ps[:], COPY, scale=rest_col[:, group : group + 1])
-                for blended_ps, first, second in (
-                    (own_ps, by_stm[:, white], by_rest[:, black]),
-                    (other_ps, by_rest[:, white], by_stm[:, black]),
-                ):
-                    nc.tensor.matmul(blended_ps[:, cols], first, identity[:], is_transpose=True, start=True, stop=False)
-                    nc.tensor.matmul(blended_ps[:, cols], second, identity[:], is_transpose=True, start=False, stop=True)
-            here = slice(n0, n0 + width)
-            clip01(nc, work, (x[:, k, here], x[:, BLOCKS + k, here]), (own_ps[:], other_ps[:]), 1.0, width)
-
-        def blend_and_clip_on_vector(k, w_acc, b_acc):
-            gap = work.tile([P, LAST], F32, name="gap")
-            nc.vector.tensor_sub(gap[:], w_acc[:], b_acc[:])
-            shift = work.tile([P, LAST], F32, name="shift")
-            nc.vector.tensor_mul(shift[:], gap[:], stm_wide[:])
-            blended = work.tile([P, 2, LAST], F32, name="blended")
-            nc.vector.tensor_add(blended[:, 0, :], b_acc[:], shift[:])
-            nc.vector.tensor_sub(blended[:, 1, :], w_acc[:], shift[:])
-            nc.vector.tensor_scalar(x[:, k : D // P : BLOCKS, B - LAST : B], blended[:], 0.0, 1.0, MAX, MIN)
-
-        def layers_and_store(n0, width, on_vector):
-            here = slice(n0, n0 + width)
-            hidden_ps = layers.tile([M, width], F32, name="hidden_ps")
+        def hidden_sums(psum, here, width):
+            hidden_ps = psum.tile([M, width], F32, name="hidden_ps")
             for j in range(D // P):
                 nc.tensor.matmul(hidden_ps[:], w1_sb[:, j, :], x[:, j, here], start=(j == 0), stop=(j == D // P - 1))
-            h = work.tile([M, width], BF16, name="h")
-            score_ps = layers.tile([1, width], F32, name="score_ps")
-            if on_vector:
-                floored = work.tile([M, width], F32, name="floored")
-                nc.vector.tensor_scalar(floored[:], hidden_ps[:], b1_sb[:, 0:1], 0.0, ADD, MAX)
-                nc.vector.tensor_scalar_min(h[:], floored[:], 1.0)
-                nc.tensor.matmul(score_ps[:], wo_sb[:, 0:1], h[:], start=True, stop=True)
-                nc.vector.tensor_scalar_add(score[:, here], score_ps[:], bo_sb[0:1, 0:1])
-            else:
+            return hidden_ps
+
+        with (
+            tc.psum_pool(name="turned", bufs=2) as turned,
+            tc.psum_pool(name="blend", bufs=2) as blend,
+            tc.psum_pool(name="layers", bufs=1) as layers,
+        ):
+            stm_ps = turned.tile([P, 2 * P], F32, name="turned_ps")
+            nc.tensor.matmul(stm_ps[:, 0:GROUPS], stm_rows[:], identity[0:GROUPS, 0:GROUPS], start=True, stop=True)
+            stm_col = held.tile([P, GROUPS], F32, name="stm_col")
+            nc.scalar.copy(stm_col[:], stm_ps[:, 0:GROUPS])
+            rest_col = held.tile([P, GROUPS], F32, name="rest_col")
+            nc.scalar.activation(rest_col[:], stm_ps[:, 0:GROUPS], IDENTITY, bias=1.0, scale=-1.0)
+
+            def blend_and_clip(k, w_acc, b_acc, n0, width):
+                own_ps = blend.tile([P, width], F32, name="own_ps")
+                other_ps = blend.tile([P, width], F32, name="other_ps")
+                for g0 in range(0, width, P):
+                    group = (n0 + g0) // P
+                    cols = slice(g0, g0 + P)
+                    white, black = slice(0, P), slice(P, 2 * P)
+                    turned_ps = turned.tile([P, 2 * P], F32, name="turned_ps")
+                    nc.tensor.transpose(turned_ps[:, white], w_acc[:, cols], identity[:])
+                    nc.tensor.transpose(turned_ps[:, black], b_acc[:, cols], identity[:])
+                    by_stm = work.tile([P, 2 * P], F32, name="by_stm")
+                    nc.scalar.activation(by_stm[:], turned_ps[:], COPY, scale=stm_col[:, group : group + 1])
+                    by_rest = work.tile([P, 2 * P], F32, name="by_rest")
+                    nc.scalar.activation(by_rest[:], turned_ps[:], COPY, scale=rest_col[:, group : group + 1])
+                    for blended_ps, first, second in (
+                        (own_ps, by_stm[:, white], by_rest[:, black]),
+                        (other_ps, by_rest[:, white], by_stm[:, black]),
+                    ):
+                        nc.tensor.matmul(
+                            blended_ps[:, cols], first, identity[:], is_transpose=True, start=True, stop=False
+                        )
+                        nc.tensor.matmul(
+                            blended_ps[:, cols], second, identity[:], is_transpose=True, start=False, stop=True
+                        )
+                here = slice(n0, n0 + width)
+                clip01(nc, work, (x[:, k, here], x[:, BLOCKS + k, here]), (own_ps[:], other_ps[:]), 1.0, width)
+
+            def layers_and_store(n0, width):
+                here = slice(n0, n0 + width)
+                hidden_ps = hidden_sums(layers, here, width)
+                h = work.tile([M, width], BF16, name="h")
                 clip01(nc, work, [h[:]], [hidden_ps[:]], one_minus_b1[:, 0:1], width)
+                score_ps = layers.tile([1, width], F32, name="score_ps")
                 nc.tensor.matmul(score_ps[:], wo_sb[:, 0:1], h[:], start=True, stop=True)
                 nc.scalar.activation(score[:, here], score_ps[:], IDENTITY, bias=bo_sb[0:1, 0:1], scale=1.0)
-            nc.sync.dma_start(out[:, here], score[:, here])
+                nc.sync.dma_start(out[:, here], score[:, here])
 
-        n0 = 0
-        for chunk in CHUNKS:
-            for k in range(BLOCKS):
-                w_acc, b_acc = gather_sums(nc, sums, windows[k], offsets, bias_wide[k], n0, chunk)
-                very_last = n0 + chunk == B and k == BLOCKS - 1
-                if very_last:
-                    blend_and_clip_on_vector(k, w_acc, b_acc)
-                for a0 in range(0, chunk, BANK):
-                    width = min(BANK, chunk - a0)
-                    piece = slice(a0, a0 + width)
-                    if not very_last:
+            n0 = 0
+            for chunk in CHUNKS:
+                for k in range(BLOCKS):
+                    w_acc, b_acc = gather_sums(nc, sums, windows[k], offsets, bias_wide[k], n0, chunk)
+                    if n0 + chunk == B and k == BLOCKS - 1:
+                        break
+                    for a0 in range(0, chunk, BANK):
+                        width = min(BANK, chunk - a0)
+                        piece = slice(a0, a0 + width)
                         blend_and_clip(k, w_acc[:, piece], b_acc[:, piece], n0 + a0, width)
-                    if k == BLOCKS - 1:
-                        layers_and_store(n0 + a0, width, very_last)
-            n0 += chunk
+                        if k == BLOCKS - 1:
+                            layers_and_store(n0 + a0, width)
+                n0 += chunk
+
+        with tc.psum_pool(name="last", bufs=LAST // P) as last:
+            k = BLOCKS - 1
+            n0 = B - LAST
+            parts = [slice(a0, a0 + P) for a0 in range(0, LAST, P)]
+            gap = work.tile([P, LAST], F32, name="gap")
+            for part in parts:
+                nc.vector.tensor_sub(gap[:, part], w_acc[:, part], b_acc[:, part])
+            shift = work.tile([P, LAST], F32, name="shift")
+            for part in parts:
+                nc.vector.tensor_mul(shift[:, part], gap[:, part], stm_wide[:, part])
+            blended = work.tile([P, 2, LAST], F32, name="blended")
+            for part in parts:
+                nc.vector.tensor_add(blended[:, 0, part], b_acc[:, part], shift[:, part])
+                nc.vector.tensor_sub(blended[:, 1, part], w_acc[:, part], shift[:, part])
+            hidden = []
+            for part in parts:
+                here = slice(n0 + part.start, n0 + part.stop)
+                nc.vector.tensor_scalar(x[:, k : D // P : BLOCKS, here], blended[:, :, part], 0.0, 1.0, MAX, MIN)
+                hidden.append(hidden_sums(last, here, P))
+            floored = work.tile([M, LAST], F32, name="floored")
+            for part, hidden_ps in zip(parts, hidden):
+                nc.vector.tensor_scalar(floored[:, part], hidden_ps[:], b1_sb[:, 0:1], 0.0, ADD, MAX)
+            h = work.tile([M, LAST], BF16, name="h")
+            scores = []
+            for part in parts:
+                nc.vector.tensor_scalar_min(h[:, part], floored[:, part], 1.0)
+                score_ps = last.tile([1, P], F32, name="score_ps")
+                nc.tensor.matmul(score_ps[:], wo_sb[:, 0:1], h[:, part], start=True, stop=True)
+                scores.append(score_ps)
+            for part, score_ps in zip(parts, scores):
+                here = slice(n0 + part.start, n0 + part.stop)
+                nc.vector.tensor_scalar_add(score[:, here], score_ps[:], bo_sb[0:1, 0:1])
+            nc.sync.dma_start(out[:, n0:B], score[:, n0:B])

@@ -76,15 +76,20 @@ def tile_halfkpnnue_kernel(tc, table, ft_bias, stm, w1, b1, wo, bo, offs, out):
         make_identity(nc, identity[:])
         one_minus_b1 = held.tile([M, 1], F32, name="one_minus_b1")
         nc.scalar.activation(one_minus_b1[:], b1_sb[:], IDENTITY, bias=1.0, scale=-1.0)
+        b1_diagonal = held.tile([M, M], F32, name="b1_diagonal")
+        nc.scalar.activation(b1_diagonal[:], identity[:], COPY, scale=b1_sb[:, 0:1])
+        ones = held.tile([M, P], F32, name="ones")
+        nc.gpsimd.memset(ones[:], 1.0)
 
         x = held.tile([P, D // P, B], BF16, name="x")
         score = held.tile([1, B], F32, name="score")
 
-        def hidden_sums(psum, here, width):
-            hidden_ps = psum.tile([M, width], F32, name="hidden_ps")
-            for j in range(D // P):
-                nc.tensor.matmul(hidden_ps[:], w1_sb[:, j, :], x[:, j, here], start=(j == 0), stop=(j == D // P - 1))
-            return hidden_ps
+        def add_to_hidden(hidden_ps, k, here, start, stop):
+            for half in range(2):
+                j = half * BLOCKS + k
+                nc.tensor.matmul(
+                    hidden_ps[:], w1_sb[:, j, :], x[:, j, here], start=(start and half == 0), stop=(stop and half == 1)
+                )
 
         with (
             tc.psum_pool(name="turned", bufs=2) as turned,
@@ -127,7 +132,9 @@ def tile_halfkpnnue_kernel(tc, table, ft_bias, stm, w1, b1, wo, bo, offs, out):
 
             def layers_and_store(n0, width):
                 here = slice(n0, n0 + width)
-                hidden_ps = hidden_sums(layers, here, width)
+                hidden_ps = layers.tile([M, width], F32, name="hidden_ps")
+                for k in range(BLOCKS):
+                    add_to_hidden(hidden_ps, k, here, k == 0, k == BLOCKS - 1)
                 h = work.tile([M, width], BF16, name="h")
                 clip01(nc, work, [h[:]], [hidden_ps[:]], one_minus_b1[:, 0:1], width)
                 score_ps = layers.tile([1, width], F32, name="score_ps")
@@ -153,6 +160,12 @@ def tile_halfkpnnue_kernel(tc, table, ft_bias, stm, w1, b1, wo, bo, offs, out):
             k = BLOCKS - 1
             n0 = B - LAST
             parts = [slice(a0, a0 + P) for a0 in range(0, LAST, P)]
+            places = [slice(n0 + part.start, n0 + part.stop) for part in parts]
+            hidden = [last.tile([M, P], F32, name="hidden_ps") for part in parts]
+            for here, hidden_ps in zip(places, hidden):
+                nc.tensor.matmul(hidden_ps[:], b1_diagonal[:], ones[:], start=True, stop=False)
+                for other_k in range(BLOCKS - 1):
+                    add_to_hidden(hidden_ps, other_k, here, False, False)
             gap = work.tile([P, LAST], F32, name="gap")
             for part in parts:
                 nc.vector.tensor_sub(gap[:, part], w_acc[:, part], b_acc[:, part])
@@ -163,22 +176,16 @@ def tile_halfkpnnue_kernel(tc, table, ft_bias, stm, w1, b1, wo, bo, offs, out):
             for part in parts:
                 nc.vector.tensor_add(blended[:, 0, part], b_acc[:, part], shift[:, part])
                 nc.vector.tensor_sub(blended[:, 1, part], w_acc[:, part], shift[:, part])
-            hidden = []
-            for part in parts:
-                here = slice(n0 + part.start, n0 + part.stop)
+            for part, here, hidden_ps in zip(parts, places, hidden):
                 nc.vector.tensor_scalar(x[:, k : D // P : BLOCKS, here], blended[:, :, part], 0.0, 1.0, MAX, MIN)
-                hidden.append(hidden_sums(last, here, P))
-            floored = work.tile([M, LAST], F32, name="floored")
-            for part, hidden_ps in zip(parts, hidden):
-                nc.vector.tensor_scalar(floored[:, part], hidden_ps[:], b1_sb[:, 0:1], 0.0, ADD, MAX)
+                add_to_hidden(hidden_ps, k, here, False, True)
             h = work.tile([M, LAST], BF16, name="h")
             scores = []
-            for part in parts:
-                nc.vector.tensor_scalar_min(h[:, part], floored[:, part], 1.0)
+            for part, hidden_ps in zip(parts, hidden):
+                nc.vector.tensor_scalar(h[:, part], hidden_ps[:], 0.0, 1.0, MAX, MIN)
                 score_ps = last.tile([1, P], F32, name="score_ps")
                 nc.tensor.matmul(score_ps[:], wo_sb[:, 0:1], h[:, part], start=True, stop=True)
                 scores.append(score_ps)
-            for part, score_ps in zip(parts, scores):
-                here = slice(n0 + part.start, n0 + part.stop)
+            for here, score_ps in zip(places, scores):
                 nc.vector.tensor_scalar_add(score[:, here], score_ps[:], bo_sb[0:1, 0:1])
             nc.sync.dma_start(out[:, n0:B], score[:, n0:B])

@@ -8,7 +8,7 @@ D, M = 2 * C, 128
 BLOCKS = C // P
 GROUPS = B // P
 BANK = 512
-CHUNKS = (1024, 640, 384)
+CHUNKS = (1152, 512, 384)
 WIDEST, LAST = CHUNKS[0], CHUNKS[-1]
 assert sum(CHUNKS) == B and all(width % P == 0 and width <= WIDEST for width in CHUNKS)
 PER_COLUMN = 16
@@ -92,7 +92,7 @@ def tile_halfkpnnue_kernel(tc, table, ft_bias, stm, w1, b1, wo, bo, offs, out):
                 )
 
         with (
-            tc.psum_pool(name="turned", bufs=2) as turned,
+            tc.psum_pool(name="turned", bufs=3) as turned,
             tc.psum_pool(name="blend", bufs=2) as blend,
             tc.psum_pool(name="layers", bufs=1) as layers,
         ):
@@ -132,12 +132,12 @@ def tile_halfkpnnue_kernel(tc, table, ft_bias, stm, w1, b1, wo, bo, offs, out):
 
             def layers_and_store(n0, width):
                 here = slice(n0, n0 + width)
-                hidden_ps = layers.tile([M, width], F32, name="hidden_ps")
+                hidden_ps = layers.tile([M, width], F32, name="hidden_ps", tag="layer_ps")
                 for k in range(BLOCKS):
                     add_to_hidden(hidden_ps, k, here, k == 0, k == BLOCKS - 1)
                 h = work.tile([M, width], BF16, name="h")
                 clip01(nc, work, [h[:]], [hidden_ps[:]], one_minus_b1[:, 0:1], width)
-                score_ps = layers.tile([1, width], F32, name="score_ps")
+                score_ps = layers.tile([1, width], F32, name="score_ps", tag="layer_ps")
                 nc.tensor.matmul(score_ps[:], wo_sb[:, 0:1], h[:], start=True, stop=True)
                 nc.scalar.activation(score[:, here], score_ps[:], IDENTITY, bias=bo_sb[0:1, 0:1], scale=1.0)
                 nc.sync.dma_start(out[:, here], score[:, here])

@@ -16,14 +16,15 @@ PER_COLUMN = 16
 FLOPS = 2 * D * M * B + 2 * M * B
 
 F32, BF16, U16 = mybir.dt.float32, mybir.dt.bfloat16, mybir.dt.uint16
-ADD, MAX, MIN = mybir.AluOpType.add, mybir.AluOpType.max, mybir.AluOpType.min
+ADD, SUBTRACT = mybir.AluOpType.add, mybir.AluOpType.subtract
+MAX, MIN = mybir.AluOpType.max, mybir.AluOpType.min
 RELU = mybir.ActivationFunctionType.Relu
 IDENTITY = mybir.ActivationFunctionType.Identity
 COPY = mybir.ActivationFunctionType.Copy
 
 
-def gather_sums(nc, sums, window, offsets, bias_wide, n0, width):
-    acc = [bias_wide, bias_wide]
+def gather_sums(nc, sums, window, offsets, zeros, n0, width):
+    acc = [zeros, zeros]
     for i in range(SLOTS_PER_SIDE):
         for side in range(2):
             first = ((side * SLOTS_PER_SIDE + i) * B + n0) // PER_COLUMN
@@ -69,9 +70,10 @@ def tile_halfkpnnue_kernel(tc, table, ft_bias, stm, w1, b1, wo, bo, offs, out):
         stm_wide = held.tile([P, LAST], F32, name="stm_wide")
         nc.sync.dma_start(stm_wide[:], stm[:, B - LAST : B].to_broadcast([P, LAST]))
 
-        bias_wide = [held.tile([P, WIDEST], F32, name=f"bias_wide{k}") for k in range(BLOCKS)]
-        for k in range(BLOCKS):
-            nc.scalar.copy(bias_wide[k][:], biases[:, k : k + 1].to_broadcast([P, WIDEST]))
+        zeros = held.tile([P, WIDEST], F32, name="zeros")
+        nc.vector.memset(zeros[:], 0.0)
+        one_minus_bias = held.tile([P, BLOCKS], F32, name="one_minus_bias")
+        nc.scalar.activation(one_minus_bias[:], biases[:], IDENTITY, bias=1.0, scale=-1.0)
         identity = held.tile([P, P], F32, name="identity")
         make_identity(nc, identity[:])
         one_minus_b1 = held.tile([M, 1], F32, name="one_minus_b1")
@@ -128,7 +130,7 @@ def tile_halfkpnnue_kernel(tc, table, ft_bias, stm, w1, b1, wo, bo, offs, out):
                             blended_ps[:, cols], second, identity[:], is_transpose=True, start=False, stop=True
                         )
                 here = slice(n0, n0 + width)
-                clip01(nc, work, (x[:, k, here], x[:, BLOCKS + k, here]), (own_ps[:], other_ps[:]), 1.0, width)
+                clip01(nc, work, (x[:, k, here], x[:, BLOCKS + k, here]), (own_ps[:], other_ps[:]), one_minus_bias[:, k : k + 1], width)
 
             def layers_and_store(n0, width):
                 here = slice(n0, n0 + width)
@@ -145,7 +147,7 @@ def tile_halfkpnnue_kernel(tc, table, ft_bias, stm, w1, b1, wo, bo, offs, out):
             n0 = 0
             for chunk in CHUNKS:
                 for k in range(BLOCKS):
-                    w_acc, b_acc = gather_sums(nc, sums, windows[k], offsets, bias_wide[k], n0, chunk)
+                    w_acc, b_acc = gather_sums(nc, sums, windows[k], offsets, zeros, n0, chunk)
                     if n0 + chunk == B and k == BLOCKS - 1:
                         break
                     for a0 in range(0, chunk, BANK):
@@ -174,8 +176,9 @@ def tile_halfkpnnue_kernel(tc, table, ft_bias, stm, w1, b1, wo, bo, offs, out):
                 nc.vector.tensor_mul(shift[:, part], gap[:, part], stm_wide[:, part])
             blended = work.tile([P, 2, LAST], F32, name="blended")
             for part in parts:
-                nc.vector.tensor_add(blended[:, 0, part], b_acc[:, part], shift[:, part])
-                nc.vector.tensor_sub(blended[:, 1, part], w_acc[:, part], shift[:, part])
+                bias = biases[:, k : k + 1]
+                nc.vector.scalar_tensor_tensor(blended[:, 0, part], b_acc[:, part], bias, shift[:, part], ADD, ADD)
+                nc.vector.scalar_tensor_tensor(blended[:, 1, part], w_acc[:, part], bias, shift[:, part], ADD, SUBTRACT)
             for part, here, hidden_ps in zip(parts, places, hidden):
                 nc.vector.tensor_scalar(x[:, k : D // P : BLOCKS, here], blended[:, :, part], 0.0, 1.0, MAX, MIN)
                 add_to_hidden(hidden_ps, k, here, False, True)

@@ -55,20 +55,20 @@ def tile_halfkpnnue_kernel(tc, table, ft_bias, stm, w1, b1, wo, bo, offs, out):
         windows = [held.tile([P, S], F32, name=f"window{k}") for k in range(BLOCKS)]
         for k in range(BLOCKS):
             nc.sync.dma_start(windows[k][:], table[k * P : (k + 1) * P, :])
-        biases = held.tile([P, BLOCKS], F32, name="biases")
-        nc.scalar.dma_start(biases[:], ft_bias.rearrange("(k p) o -> p (k o)", p=P))
         stm_rows = held.tile([GROUPS, P], F32, name="stm_rows")
-        nc.scalar.dma_start(stm_rows[:], stm.rearrange("o (g p) -> (o g) p", p=P))
+        nc.sync.dma_start(stm_rows[:], stm.rearrange("o (g p) -> (o g) p", p=P))
         w1_sb = held.tile([P, D // P, M], BF16, name="w1_sb")
         nc.sync.dma_start(w1_sb[:], w1.rearrange("(j p) m -> p j m", p=P))
-        b1_sb = held.tile([M, 1], F32, name="b1_sb")
-        nc.scalar.dma_start(b1_sb[:], b1)
-        wo_sb = held.tile([M, 1], BF16, name="wo_sb")
-        nc.scalar.dma_start(wo_sb[:], wo)
-        bo_sb = held.tile([1, 1], F32, name="bo_sb")
-        nc.scalar.dma_start(bo_sb[:], bo)
         stm_wide = held.tile([P, LAST], F32, name="stm_wide")
         nc.sync.dma_start(stm_wide[:], stm[:, B - LAST : B].to_broadcast([P, LAST]))
+        biases = held.tile([P, BLOCKS], F32, name="biases")
+        nc.sync.dma_start(biases[:], ft_bias.rearrange("(k p) o -> p (k o)", p=P))
+        b1_sb = held.tile([M, 1], F32, name="b1_sb")
+        nc.sync.dma_start(b1_sb[:], b1)
+        wo_sb = held.tile([M, 1], BF16, name="wo_sb")
+        nc.sync.dma_start(wo_sb[:], wo)
+        bo_sb = held.tile([1, 1], F32, name="bo_sb")
+        nc.sync.dma_start(bo_sb[:], bo)
 
         zeros = held.tile([P, WIDEST], F32, name="zeros")
         nc.vector.memset(zeros[:], 0.0)

@@ -12,6 +12,8 @@ CHUNKS = (1152, 512, 384)
 WIDEST, LAST = CHUNKS[0], CHUNKS[-1]
 assert sum(CHUNKS) == B and all(width % P == 0 and width <= WIDEST for width in CHUNKS)
 PER_COLUMN = 16
+ROW_TILE = 32
+BF16_PIECES = 3
 
 FLOPS = 2 * D * M * B + 2 * M * B
 
@@ -78,9 +80,22 @@ def tile_halfkpnnue_kernel(tc, table, ft_bias, stm, w1, b1, wo, bo, offs, out):
         make_identity(nc, identity[:])
         one_minus_b1 = held.tile([M, 1], F32, name="one_minus_b1")
         nc.scalar.activation(one_minus_b1[:], b1_sb[:], IDENTITY, bias=1.0, scale=-1.0)
-        b1_diagonal = held.tile([M, M], F32, name="b1_diagonal")
-        nc.scalar.activation(b1_diagonal[:], identity[:], COPY, scale=b1_sb[:, 0:1])
-        ones = held.tile([M, P], F32, name="ones")
+        b1_pieces = held.tile([M, ROW_TILE], F32, name="b1_pieces")
+        nc.gpsimd.memset(b1_pieces[:], 0.0)
+        rest = b1_sb
+        for i in range(BF16_PIECES):
+            piece = held.tile([M, 1], BF16, name=f"b1_piece{i}")
+            nc.scalar.copy(piece[:], rest[:])
+            nc.scalar.copy(b1_pieces[:, i : i + 1], piece[:])
+            if i == BF16_PIECES - 1:
+                break
+            minus_piece = held.tile([M, 1], F32, name=f"minus_b1_piece{i}")
+            nc.scalar.mul(minus_piece[:], piece[:], -1.0)
+            smaller_rest = held.tile([M, 1], F32, name=f"b1_rest{i}")
+            nc.scalar.activation(smaller_rest[:], rest[:], IDENTITY, bias=minus_piece[:, 0:1], scale=1.0)
+            rest = smaller_rest
+        b1_rows = held.tile([ROW_TILE, M], BF16, name="b1_rows")
+        ones = held.tile([ROW_TILE, P], BF16, name="ones")
         nc.gpsimd.memset(ones[:], 1.0)
 
         x = held.tile([P, D // P, B], BF16, name="x")
@@ -104,6 +119,9 @@ def tile_halfkpnnue_kernel(tc, table, ft_bias, stm, w1, b1, wo, bo, offs, out):
             nc.scalar.copy(stm_col[:], stm_ps[:, 0:GROUPS])
             rest_col = held.tile([P, GROUPS], F32, name="rest_col")
             nc.scalar.activation(rest_col[:], stm_ps[:, 0:GROUPS], IDENTITY, bias=1.0, scale=-1.0)
+            b1_rows_ps = turned.tile([ROW_TILE, M], F32, name="b1_rows_ps", tag="turned_ps")
+            nc.tensor.transpose(b1_rows_ps[:], b1_pieces[:], identity[:])
+            nc.scalar.copy(b1_rows[:], b1_rows_ps[:])
 
             def blend_and_clip(k, w_acc, b_acc, n0, width):
                 own_ps = blend.tile([P, width], F32, name="own_ps")
@@ -165,7 +183,7 @@ def tile_halfkpnnue_kernel(tc, table, ft_bias, stm, w1, b1, wo, bo, offs, out):
             places = [slice(n0 + part.start, n0 + part.stop) for part in parts]
             hidden = [last.tile([M, P], F32, name="hidden_ps") for part in parts]
             for here, hidden_ps in zip(places, hidden):
-                nc.tensor.matmul(hidden_ps[:], b1_diagonal[:], ones[:], start=True, stop=False)
+                nc.tensor.matmul(hidden_ps[:], b1_rows[:], ones[:], start=True, stop=False)
                 for other_k in range(BLOCKS - 1):
                     add_to_hidden(hidden_ps, other_k, here, False, False)
             gap = work.tile([P, LAST], F32, name="gap")

import concourse.mybir as mybir
from concourse.masks import make_identity

P = 128
C, S, B = 256, 2048, 2048
SLOTS_PER_SIDE = 4
D, M = 2 * C, 128
BLOCKS = C // P
GROUPS = B // P
BANK = 512
CHUNKS = (1152, 512, 384)
WIDEST, LAST = CHUNKS[0], CHUNKS[-1]
assert sum(CHUNKS) == B and all(width % P == 0 and width <= WIDEST for width in CHUNKS)
PER_COLUMN = 16
ROW_TILE = 32
BF16_PIECES = 3

FLOPS = 2 * D * M * B + 2 * M * B

F32, BF16, U16 = mybir.dt.float32, mybir.dt.bfloat16, mybir.dt.uint16
ADD, SUBTRACT = mybir.AluOpType.add, mybir.AluOpType.subtract
MAX, MIN = mybir.AluOpType.max, mybir.AluOpType.min
RELU = mybir.ActivationFunctionType.Relu
IDENTITY = mybir.ActivationFunctionType.Identity
COPY = mybir.ActivationFunctionType.Copy


def gather_sums(nc, sums, window, offsets, zeros, n0, width):
    acc = [zeros, zeros]
    for i in range(SLOTS_PER_SIDE):
        for side in range(2):
            first = ((side * SLOTS_PER_SIDE + i) * B + n0) // PER_COLUMN
            picked = window[:].indirect(offsets[:, first : first + width // PER_COLUMN])
            summed = sums.tile([P, width], F32, name="summed")
            nc.vector.tensor_tensor(summed[:], picked, acc[side][:, :width], ADD)
            acc[side] = summed
    return acc


def clip01(nc, work, clipped, values, one_minus_bias, width):
    aboves = [work.tile([P, width], F32, name="above") for value in values]
    for above, value in zip(aboves, values):
        nc.scalar.activation(above[:], value, RELU, bias=one_minus_bias, scale=-1.0)
    for above, result in zip(aboves, clipped):
        nc.scalar.activation(result, above[:], RELU, bias=1.0, scale=-1.0)


def tile_halfkpnnue_kernel(tc, table, ft_bias, stm, w1, b1, wo, bo, offs, out):
    nc = tc.nc
    with (
        tc.tile_pool(name="held", bufs=1) as held,
        tc.tile_pool(name="sums", bufs=12) as sums,
        tc.tile_pool(name="work", bufs=4) as work,
    ):
        offsets = held.tile([P, offs.shape[1]], U16, name="offsets")
        nc.sync.dma_start(offsets[:], offs)
        windows = [held.tile([P, S], F32, name=f"window{k}") for k in range(BLOCKS)]
        for k in range(BLOCKS):
            nc.sync.dma_start(windows[k][:], table[k * P : (k + 1) * P, :])
        stm_rows = held.tile([GROUPS, P], F32, name="stm_rows")
        nc.sync.dma_start(stm_rows[:], stm.rearrange("o (g p) -> (o g) p", p=P))
        w1_sb = held.tile([P, D // P, M], BF16, name="w1_sb")
        nc.sync.dma_start(w1_sb[:], w1.rearrange("(j p) m -> p j m", p=P))
        stm_wide = held.tile([P, LAST], F32, name="stm_wide")
        nc.sync.dma_start(stm_wide[:], stm[:, B - LAST : B].to_broadcast([P, LAST]))
        biases = held.tile([P, BLOCKS], F32, name="biases")
        nc.sync.dma_start(biases[:], ft_bias.rearrange("(k p) o -> p (k o)", p=P))
        b1_sb = held.tile([M, 1], F32, name="b1_sb")
        nc.sync.dma_start(b1_sb[:], b1)
        wo_sb = held.tile([M, 1], BF16, name="wo_sb")
        nc.sync.dma_start(wo_sb[:], wo)
        bo_sb = held.tile([1, 1], F32, name="bo_sb")
        nc.sync.dma_start(bo_sb[:], bo)

        zeros = held.tile([P, WIDEST], F32, name="zeros")
        nc.vector.memset(zeros[:], 0.0)
        one_minus_bias = held.tile([P, BLOCKS], F32, name="one_minus_bias")
        nc.scalar.activation(one_minus_bias[:], biases[:], IDENTITY, bias=1.0, scale=-1.0)
        identity = held.tile([P, P], F32, name="identity")
        make_identity(nc, identity[:])
        one_minus_b1 = held.tile([M, 1], F32, name="one_minus_b1")
        nc.scalar.activation(one_minus_b1[:], b1_sb[:], IDENTITY, bias=1.0, scale=-1.0)
        b1_pieces = held.tile([M, ROW_TILE], F32, name="b1_pieces")
        nc.gpsimd.memset(b1_pieces[:], 0.0)
        rest = b1_sb
        for i in range(BF16_PIECES):
            piece = held.tile([M, 1], BF16, name=f"b1_piece{i}")
            nc.scalar.copy(piece[:], rest[:])
            nc.scalar.copy(b1_pieces[:, i : i + 1], piece[:])
            if i == BF16_PIECES - 1:
                break
            minus_piece = held.tile([M, 1], F32, name=f"minus_b1_piece{i}")
            nc.scalar.mul(minus_piece[:], piece[:], -1.0)
            smaller_rest = held.tile([M, 1], F32, name=f"b1_rest{i}")
            nc.scalar.activation(smaller_rest[:], rest[:], IDENTITY, bias=minus_piece[:, 0:1], scale=1.0)
            rest = smaller_rest
        b1_rows = held.tile([ROW_TILE, M], BF16, name="b1_rows")
        ones = held.tile([ROW_TILE, P], BF16, name="ones")
        nc.gpsimd.memset(ones[:], 1.0)

        x = held.tile([P, D // P, B], BF16, name="x")
        score = held.tile([1, B], F32, name="score")

        def add_to_hidden(hidden_ps, k, here, start, stop):
            for half in range(2):
                j = half * BLOCKS + k
                nc.tensor.matmul(
                    hidden_ps[:], w1_sb[:, j, :], x[:, j, here], start=(start and half == 0), stop=(stop and half == 1)
                )

        with (
            tc.psum_pool(name="turned", bufs=3) as turned,
            tc.psum_pool(name="blend", bufs=2) as blend,
            tc.psum_pool(name="layers", bufs=1) as layers,
        ):
            stm_ps = turned.tile([P, 2 * P], F32, name="turned_ps")
            nc.tensor.matmul(stm_ps[:, 0:GROUPS], stm_rows[:], identity[0:GROUPS, 0:GROUPS], start=True, stop=True)
            stm_col = held.tile([P, GROUPS], F32, name="stm_col")
            nc.scalar.copy(stm_col[:], stm_ps[:, 0:GROUPS])
            rest_col = held.tile([P, GROUPS], F32, name="rest_col")
            nc.scalar.activation(rest_col[:], stm_ps[:, 0:GROUPS], IDENTITY, bias=1.0, scale=-1.0)
            b1_rows_ps = turned.tile([ROW_TILE, M], F32, name="b1_rows_ps", tag="turned_ps")
            nc.tensor.transpose(b1_rows_ps[:], b1_pieces[:], identity[:])
            nc.scalar.copy(b1_rows[:], b1_rows_ps[:])

            def blend_and_clip(k, w_acc, b_acc, n0, width):
                own_ps = blend.tile([P, width], F32, name="own_ps")
                other_ps = blend.tile([P, width], F32, name="other_ps")
                for g0 in range(0, width, P):
                    group = (n0 + g0) // P
                    cols = slice(g0, g0 + P)
                    white, black = slice(0, P), slice(P, 2 * P)
                    turned_ps = turned.tile([P, 2 * P], F32, name="turned_ps")
                    nc.tensor.transpose(turned_ps[:, white], w_acc[:, cols], identity[:])
                    nc.tensor.transpose(turned_ps[:, black], b_acc[:, cols], identity[:])
                    by_stm = work.tile([P, 2 * P], F32, name="by_stm")
                    nc.scalar.activation(by_stm[:], turned_ps[:], COPY, scale=stm_col[:, group : group + 1])
                    by_rest = work.tile([P, 2 * P], F32, name="by_rest")
                    nc.scalar.activation(by_rest[:], turned_ps[:], COPY, scale=rest_col[:, group : group + 1])
                    for blended_ps, first, second in (
                        (own_ps, by_stm[:, white], by_rest[:, black]),
                        (other_ps, by_rest[:, white], by_stm[:, black]),
                    ):
                        nc.tensor.matmul(
                            blended_ps[:, cols], first, identity[:], is_transpose=True, start=True, stop=False
                        )
                        nc.tensor.matmul(
                            blended_ps[:, cols], second, identity[:], is_transpose=True, start=False, stop=True
                        )
                here = slice(n0, n0 + width)
                clip01(nc, work, (x[:, k, here], x[:, BLOCKS + k, here]), (own_ps[:], other_ps[:]), one_minus_bias[:, k : k + 1], width)

            def layers_and_store(n0, width):
                here = slice(n0, n0 + width)
                hidden_ps = layers.tile([M, width], F32, name="hidden_ps", tag="layer_ps")
                for k in range(BLOCKS):
                    add_to_hidden(hidden_ps, k, here, k == 0, k == BLOCKS - 1)
                h = work.tile([M, width], BF16, name="h")
                clip01(nc, work, [h[:]], [hidden_ps[:]], one_minus_b1[:, 0:1], width)
                score_ps = layers.tile([1, width], F32, name="score_ps", tag="layer_ps")
                nc.tensor.matmul(score_ps[:], wo_sb[:, 0:1], h[:], start=True, stop=True)
                nc.scalar.activation(score[:, here], score_ps[:], IDENTITY, bias=bo_sb[0:1, 0:1], scale=1.0)
                nc.sync.dma_start(out[:, here], score[:, here])

            n0 = 0
            for chunk in CHUNKS:
                for k in range(BLOCKS):
                    w_acc, b_acc = gather_sums(nc, sums, windows[k], offsets, zeros, n0, chunk)
                    if n0 + chunk == B and k == BLOCKS - 1:
                        break
                    for a0 in range(0, chunk, BANK):
                        width = min(BANK, chunk - a0)
                        piece = slice(a0, a0 + width)
                        blend_and_clip(k, w_acc[:, piece], b_acc[:, piece], n0 + a0, width)
                        if k == BLOCKS - 1:
                            layers_and_store(n0 + a0, width)
                n0 += chunk

        with tc.psum_pool(name="last", bufs=LAST // P) as last:
            k = BLOCKS - 1
            n0 = B - LAST
            parts = [slice(a0, a0 + P) for a0 in range(0, LAST, P)]
            places = [slice(n0 + part.start, n0 + part.stop) for part in parts]
            hidden = [last.tile([M, P], F32, name="hidden_ps") for part in parts]
            for here, hidden_ps in zip(places, hidden):
                nc.tensor.matmul(hidden_ps[:], b1_rows[:], ones[:], start=True, stop=False)
                for other_k in range(BLOCKS - 1):
                    add_to_hidden(hidden_ps, other_k, here, False, False)
            gap = work.tile([P, LAST], F32, name="gap")
            for part in parts:
                nc.vector.tensor_sub(gap[:, part], w_acc[:, part], b_acc[:, part])
            shift = work.tile([P, LAST], F32, name="shift")
            for part in parts:
                nc.vector.tensor_mul(shift[:, part], gap[:, part], stm_wide[:, part])
            blended = work.tile([P, 2, LAST], F32, name="blended")
            for part in parts:
                bias = biases[:, k : k + 1]
                nc.vector.scalar_tensor_tensor(blended[:, 0, part], b_acc[:, part], bias, shift[:, part], ADD, ADD)
                nc.vector.scalar_tensor_tensor(blended[:, 1, part], w_acc[:, part], bias, shift[:, part], ADD, SUBTRACT)
            for part, here, hidden_ps in zip(parts, places, hidden):
                nc.vector.tensor_scalar(x[:, k : D // P : BLOCKS, here], blended[:, :, part], 0.0, 1.0, MAX, MIN)
                add_to_hidden(hidden_ps, k, here, False, True)
            h = work.tile([M, LAST], BF16, name="h")
            scores = []
            for part, hidden_ps in zip(parts, hidden):
                nc.vector.tensor_scalar(h[:, part], hidden_ps[:], 0.0, 1.0, MAX, MIN)
                score_ps = last.tile([1, P], F32, name="score_ps")
                nc.tensor.matmul(score_ps[:], wo_sb[:, 0:1], h[:, part], start=True, stop=True)
                scores.append(score_ps)
            for here, score_ps in zip(places, scores):
                nc.vector.tensor_scalar_add(score[:, here], score_ps[:], bo_sb[0:1, 0:1])
            nc.sync.dma_start(out[:, n0:B], score[:, n0:B])
